import numpy as np
import ml_dtypes


def mxq(x, axis, fmt="e4m3"):
    dtype, down = {"e4m3": (ml_dtypes.float8_e4m3fn, 7), "e5m2": (ml_dtypes.float8_e5m2, 14)}[fmt]
    v = np.moveaxis(np.asarray(x, np.float32).astype(ml_dtypes.bfloat16).astype(np.float64), axis, -1)
    blocks = v.reshape(v.shape[:-1] + (-1, 32))
    amax = np.abs(blocks).max(-1, keepdims=True)
    byte = np.maximum(np.where(amax > 0, np.frexp(amax)[1] - 1 + 127, 0) - down, 1)
    scale = np.exp2(byte - 127.0)
    codes = (blocks / scale).astype(np.float32).astype(dtype).astype(np.float64)
    return np.moveaxis((codes * scale).reshape(v.shape), -1, axis)


WIDE = False


def mx_kscale(k):
    if not WIDE:
        return np.ones(k)
    levels = np.array([10, -10, 5, -5, 0])
    a = np.random.permutation(np.resize(levels, k // 512 * 4)).reshape(k // 512, 4)
    idx = np.arange(k)
    return np.exp2(a[idx // 512, idx % 128 // 32])


BF16 = ml_dtypes.bfloat16


def bf(x):
    return np.asarray(x, np.float32).astype(BF16)


def f64(x):
    return np.asarray(x).astype(np.float64)


B, T, C, QLR, H, R, KVL, VD = 4, 1024, 1024, 1536, 4, 128, 512, 128
THETA = 10000.0
EPS = 1e-6
HALF = R // 2


def rms_norm(v, w):
    return v / np.sqrt(np.mean(v * v, axis=-1, keepdims=True) + EPS) * w


def rope_cos_sin():
    inv = 1.0 / THETA ** (np.arange(HALF) / HALF)
    ang = np.arange(T)[:, None] * inv
    return np.cos(ang), np.sin(ang)


def apply_rot(v, cos, sin):
    vr, vi = v[..., 0::2], v[..., 1::2]
    c = cos[None, :, None, :]
    s = sin[None, :, None, :]
    return np.stack([vr * c - vi * s, vr * s + vi * c], axis=-1).reshape(v.shape)


def setup_inputs():
    s, t = mx_kscale(C), mx_kscale(KVL)
    return {"x": bf(np.random.standard_normal((B, T, C)) * s),
            "w_kva": bf(np.random.standard_normal((KVL + R, C)) / np.sqrt(C) / s),
            "kva_norm_w": bf((1.0 + 0.1 * np.random.standard_normal(KVL)) * t),
            "w_kvb": bf(np.random.standard_normal((H * (R + VD), KVL)) / np.sqrt(KVL) / t)}


def reference(x, w_kva, kva_norm_w, w_kvb):
    kv_a = mxq(f64(x), 2, "e4m3") @ mxq(f64(w_kva), 1, "e4m3").T
    kv_c = rms_norm(kv_a[..., :KVL], f64(kva_norm_w))
    k_rope_raw = kv_a[..., KVL:]
    kv = (mxq(kv_c, 2, "e4m3") @ mxq(f64(w_kvb), 1, "e4m3").T).reshape(B, T, H, R + VD)
    k_content, v = kv[..., :R], kv[..., R:]
    k_rope = np.broadcast_to(k_rope_raw[:, :, None, :], (B, T, H, R))
    cos, sin = rope_cos_sin()
    k = np.concatenate([k_content, apply_rot(k_rope, cos, sin)], axis=-1)
    return k, v

@@ -1,0 +1,380 @@
+import math
+
+import concourse.mybir as mybir
+from concourse.masks import make_identity
+
+F32 = mybir.dt.float32
+BF16 = mybir.dt.bfloat16
+I32 = mybir.dt.int32
+U32 = mybir.dt.uint32
+U8 = mybir.dt.uint8
+FP8X4 = mybir.dt.float8_e4m3fn_x4
+ALU = mybir.AluOpType
+ACT = mybir.ActivationFunctionType
+
+P = 128
+B, T, C = 4, 1024, 1024
+KVL, R, H = 512, 128, 4
+TPP = 8
+N_PAIRS = B * TPP // 2
+N_QUADS = N_PAIRS // 2
+EPS = 1e-6
+RATIO = 10000.0 ** (-1.0 / 64.0)
+PAIR_STORES_FROM = 12
+
+FLOPS = 2 * B * T * C * (KVL + R) + 2 * B * T * KVL * (H * 256)
+
+
+def tile_multiheadlatentattention_pb_t_kernel(tc, x, w_kva, kva_norm_w, w_kvb, out_0, out_1):
+    nc = tc.nc
+    with tc.tile_pool(name="const", bufs=1) as const, tc.tile_pool(name="xin", bufs=8) as xin, tc.tile_pool(
+        name="stage", bufs=3
+    ) as stage, tc.tile_pool(name="ring", bufs=7) as ring, tc.tile_pool(name="work", bufs=3) as work, tc.tile_pool(
+        name="small", bufs=4
+    ) as small, tc.psum_pool(name="psum", bufs=1) as psum, tc.manual_schedule():
+        state = {"k": 0}
+
+        def k_bank(shape, dtype, name):
+            tag = "K%d" % (state["k"] % 4)
+            state["k"] = state["k"] + 1
+            return psum.tile(shape, dtype, name=name, tag=tag)
+
+        engines = {"S": nc.scalar.copy, "V": nc.vector.tensor_copy}
+
+        g_bc = const.tile([P, KVL], BF16, name="g_bc")
+        nc.scalar.dma_start(out=g_bc[:], in_=kva_norm_w.partition_broadcast(P))
+
+        waq = const.tile([P, 2 * 640], U32, name="waq", align_bytes=64)
+        was = const.tile([P, 2 * 640], U8, name="was", align_bytes=64)
+        wbq = const.tile([P, 1024], U32, name="wbq", align_bytes=64)
+        wbs = const.tile([P, 1024], U8, name="wbs", align_bytes=64)
+        tab1 = const.tile([P, TPP, 2, 64], F32, name="tab1")
+        tab2 = const.tile([P, TPP, 2, 64], F32, name="tab2")
+        ident_f = const.tile([P, P], F32, name="ident_f")
+        ident_b = const.tile([P, P], BF16, name="ident_b")
+        eps_t = const.tile([P, 1], F32, name="eps_t")
+
+        x_rows = x.rearrange("b (p t) k -> b p (t k)", t=TPP)
+        k_rows = out_0.rearrange("b (p t) h d -> b p t (h d)", t=TPP)
+        v_rows = out_1.rearrange("b (p t) h d -> b p t (h d)", t=TPP)
+        x_words = []
+        live = {}
+
+        def transpose_words(src_words):
+            xt = k_bank([P, 512], F32, "xt")
+            for c in range(4):
+                nc.tensor.transpose(
+                    out=xt[:, P * c : P * c + P], in_=src_words[:, P * c : P * c + P], identity=ident_f[:]
+                )
+            return xt
+
+        def copy_words(xt, dst_bf16, eng):
+            engines[eng](
+                out=dst_bf16.bitcast(F32).rearrange("p (g w u) -> p g w u", g=2, u=2),
+                in_=xt[:].rearrange("p (g u w) -> p g w u", g=2, u=2),
+            )
+
+        with tc.tile_pool(name="setup", bufs=1) as setup:
+            war = setup.tile([P, 5 * C], BF16, name="war")
+            nc.sync.dma_start(
+                out=war[:].rearrange("p (r k) -> p r k", r=5), in_=w_kva.rearrange("(r p) k -> p r k", p=P)
+            )
+            wbr = setup.tile([P, 8 * KVL], BF16, name="wbr")
+            nc.sync.dma_start(
+                out=wbr[:].rearrange("p (r k) -> p r k", r=8), in_=w_kvb.rearrange("(r p) k -> p r k", p=P)
+            )
+            for hb in range(8):
+                xr = xin.tile([P, 4 * C], BF16, name="xr", tag="xr")
+                nc.sync.dma_start(out=xr[:], in_=x_rows[hb // 2][:, 4 * C * (hb % 2) : 4 * C * (hb % 2) + 4 * C])
+                x_words.append(xr[:].bitcast(F32))
+
+            pos_i = setup.tile([P, TPP], I32, name="pos_i")
+            nc.gpsimd.iota(pos_i[:], pattern=[[1, TPP]], base=0, channel_multiplier=TPP)
+            make_identity(nc, ident_f[:])
+            make_identity(nc, ident_b[:])
+            nc.vector.memset(eps_t[:], EPS)
+            pos_f = setup.tile([P, TPP], F32, name="pos_f")
+            nc.vector.tensor_copy(out=pos_f[:], in_=pos_i[:])
+            inv = setup.tile([P, 64], F32, name="inv")
+            nc.vector.memset(inv[:, 0:1], 1.0)
+            for s in range(6):
+                n = 2**s
+                nc.vector.tensor_scalar(
+                    out=inv[:, n : 2 * n], in0=inv[:, 0:n], scalar1=RATIO**n, scalar2=None, op0=ALU.mult
+                )
+            turns = setup.tile([P, TPP, 64], F32, name="turns")
+            nc.vector.scalar_tensor_tensor(
+                out=turns[:],
+                in0=pos_f[:].unsqueeze(2).to_broadcast([P, TPP, 64]),
+                scalar=1.0 / (2.0 * math.pi),
+                in1=inv[:].unsqueeze(1).to_broadcast([P, TPP, 64]),
+                op0=ALU.mult,
+                op1=ALU.mult,
+            )
+            whole_i = setup.tile([P, TPP, 64], I32, name="whole_i")
+            nc.vector.tensor_copy(out=whole_i[:], in_=turns[:])
+            whole_f = setup.tile([P, TPP, 64], F32, name="whole_f")
+            nc.vector.tensor_copy(out=whole_f[:], in_=whole_i[:])
+            frac = setup.tile([P, TPP, 64], F32, name="frac")
+            nc.vector.tensor_tensor(out=frac[:], in0=turns[:], in1=whole_f[:], op=ALU.subtract)
+            sin_h = setup.tile([P, TPP, 64], F32, name="sin_h")
+            nc.scalar.activation(out=sin_h[:], in_=frac[:], func=ACT.Sin, scale=math.pi)
+            sin_q = setup.tile([P, TPP, 64], F32, name="sin_q")
+            nc.scalar.activation(out=sin_q[:], in_=frac[:], func=ACT.Sin, scale=0.5 * math.pi)
+            sq_q = setup.tile([P, TPP, 64], F32, name="sq_q")
+            nc.gpsimd.tensor_tensor(out=sq_q[:], in0=sin_q[:], in1=sin_q[:], op=ALU.mult)
+            cos_h = setup.tile([P, TPP, 64], F32, name="cos_h")
+            nc.gpsimd.tensor_scalar(
+                out=cos_h[:], in0=sq_q[:], scalar1=-2.0, scalar2=1.0, op0=ALU.mult, op1=ALU.add
+            )
+            prod = setup.tile([P, TPP, 64], F32, name="prod")
+            nc.gpsimd.tensor_tensor(out=prod[:], in0=sin_h[:], in1=cos_h[:], op=ALU.mult)
+            nc.gpsimd.tensor_scalar(
+                out=tab1[:, :, 1, :], in0=prod[:], scalar1=2.0, scalar2=0.0, op0=ALU.mult, op1=ALU.add
+            )
+            nc.gpsimd.tensor_scalar(
+                out=tab2[:, :, 0, :], in0=prod[:], scalar1=-2.0, scalar2=0.0, op0=ALU.mult, op1=ALU.add
+            )
+            sq_h = setup.tile([P, TPP, 64], F32, name="sq_h")
+            nc.gpsimd.tensor_tensor(out=sq_h[:], in0=sin_h[:], in1=sin_h[:], op=ALU.mult)
+            nc.gpsimd.tensor_scalar(
+                out=tab1[:, :, 0, :], in0=sq_h[:], scalar1=-2.0, scalar2=1.0, op0=ALU.mult, op1=ALU.add
+            )
+            nc.gpsimd.tensor_scalar(
+                out=tab2[:, :, 1, :], in0=sq_h[:], scalar1=-2.0, scalar2=1.0, op0=ALU.mult, op1=ALU.add
+            )
+
+            war_w = war[:].bitcast(F32)
+            for r in range(5):
+                xt = transpose_words(war_w[:, 512 * r : 512 * r + 512])
+                grp = stage.tile([P, 1024], BF16, name="grp", tag="cgrp", align_bytes=64)
+                copy_words(xt, grp[:], "SV"[r % 2])
+                for g in range(2):
+                    cols = slice(640 * g + P * r, 640 * g + P * r + P)
+                    nc.vector.quantize_mx(
+                        out=waq[:, cols].bitcast(FP8X4), scales=was[:, cols], in_=grp[:, 512 * g : 512 * g + 512]
+                    )
+            for n, (ra, rb, dest) in enumerate(((0, 2, 0), (4, 6, 256), (1, 3, 512), (5, 7, 768))):
+                wt = k_bank([P, 2, 4, P], BF16, "wt")
+                for a, r in enumerate((ra, rb)):
+                    for j in range(4):
+                        nc.tensor.transpose(
+                            out=wt[:, a, j, :],
+                            in_=wbr[:, KVL * r + P * j : KVL * r + P * j + P],
+                            identity=ident_b[:],
+                        )
+                grp = stage.tile([P, 1024], BF16, name="grp", tag="cgrp", align_bytes=64)
+                engines["VS"[n % 2]](
+                    out=grp[:].rearrange("p (a w j) -> p a w j", a=2, j=4),
+                    in_=wt[:].rearrange("p a j w -> p a w j"),
+                )
+                nc.vector.quantize_mx(
+                    out=wbq[:, dest : dest + 256].bitcast(FP8X4), scales=wbs[:, dest : dest + 256], in_=grp[:]
+                )
+
+        def x_transpose(q):
+            live["xt", q] = [
+                transpose_words(x_words[(2 * q + a) // 4][:, 512 * ((2 * q + a) % 4) : 512 * ((2 * q + a) % 4) + 512])
+                for a in range(2)
+            ]
+
+        def x_copy(q):
+            xg = stage.tile([P, 2048], BF16, name="xg", tag="xgrp", align_bytes=64)
+            for a in range(2):
+                copy_words(live["xt", q][a], xg[:, 1024 * a : 1024 * a + 1024], "SV"[a])
+            live["xg", q] = xg
+
+        def x_quantise(q):
+            xq = ring.tile([P, 512], U32, name="xq", tag="xq", align_bytes=64)
+            xs = ring.tile([P, 512], U8, name="xs", tag="xs", align_bytes=64)
+            nc.vector.quantize_mx(out=xq[:].bitcast(FP8X4), scales=xs[:], in_=live["xg", q][:])
+            live["xq", q] = (xq, xs)
+
+        def stage1_pass(out, q, a, g, lo, hi):
+            xq, xs = live["xq", q]
+            xc = slice(256 * a + P * g, 256 * a + P * g + P)
+            nc.tensor.matmul_mx(
+                out=out,
+                lhsT=xq[:, xc].bitcast(FP8X4),
+                lhsT_scale=xs[:, xc],
+                rhs=waq[:, 640 * g + lo : 640 * g + hi].bitcast(FP8X4),
+                rhs_scale=was[:, 640 * g + lo : 640 * g + hi],
+                start=(g == 0),
+                stop=(g == 1),
+            )
+
+        def stage1_latent(q):
+            tiles = []
+            for a in range(2):
+                l = psum.tile([P, KVL], F32, name="l", tag="L%d" % a)
+                for g in range(2):
+                    stage1_pass(l[:], q, a, g, 0, KVL)
+                tiles.append(l)
+            live["l", q] = tiles
+
+        def stage1_rotary(quad):
+            r_ps = psum.tile([P, 4, R], F32, name="r_ps", tag="R")
+            for tt in range(4):
+                for g in range(2):
+                    stage1_pass(r_ps[:, tt, :], 2 * quad + tt // 2, tt % 2, g, KVL, KVL + R)
+            live["r", quad] = r_ps
+
+        def squares(q):
+            ssq = small.tile([P, 2], F32, name="ssq", tag="ssq")
+            for a in range(2):
+                junk = work.tile([P, KVL], BF16, name="junk", tag="junk", bufs=2)
+                nc.scalar.activation(out=junk[:], in_=live["l", q][a][:], func=ACT.Square, accum_out=ssq[:, a : a + 1])
+            std = small.tile([P, 2], F32, name="std", tag="std")
+            nc.scalar.activation(out=std[:], in_=ssq[:], func=ACT.Sqrt, scale=1.0 / KVL, bias=eps_t[:, 0:1])
+            live["std", q] = std
+
+        def normalise(q):
+            rstd = small.tile([P, 2], F32, name="rstd", tag="rstd")
+            nc.vector.reciprocal(out=rstd[:], in_=live["std", q][:])
+            c_sb = work.tile([P, 2, KVL], BF16, name="c_sb", tag="c_sb")
+            for a in range(2):
+                nc.vector.scalar_tensor_tensor(
+                    out=c_sb[:, a, :],
+                    in0=live["l", q][a][:],
+                    scalar=rstd[:, a : a + 1],
+                    in1=g_bc[:],
+                    op0=ALU.mult,
+                    op1=ALU.mult,
+                )
+            live["c", q] = c_sb
+
+        def c_transpose(q):
+            ct = psum.tile([P, 2, 4, P], BF16, name="ct", tag="C")
+            for a in range(2):
+                for j in range(4):
+                    nc.tensor.transpose(
+                        out=ct[:, a, j, :], in_=live["c", q][:, a, P * j : P * j + P], identity=ident_b[:]
+                    )
+            live["ct", q] = ct
+
+        def c_copy(q):
+            grp = stage.tile([P, 1024], BF16, name="grp", tag="cgrp", align_bytes=64)
+            nc.scalar.copy(
+                out=grp[:].rearrange("p (a w j) -> p a w j", a=2, j=4),
+                in_=live["ct", q][:].rearrange("p a j w -> p a w j"),
+            )
+            live["cg", q] = grp
+
+        def c_quantise(q):
+            cq = work.tile([P, 256], U32, name="cq", tag="cq", align_bytes=64)
+            cs = work.tile([P, 256], U8, name="cs", tag="cs", align_bytes=64)
+            nc.vector.quantize_mx(out=cq[:].bitcast(FP8X4), scales=cs[:], in_=live["cg", q][:])
+            live["cq", q] = (cq, cs)
+
+        def stage2(q):
+            cq, cs = live["cq", q]
+            banks = []
+            for a in range(2):
+                for part in range(2):
+                    kv = k_bank([P, 512], F32, "kv")
+                    nc.tensor.matmul_mx(
+                        out=kv[:],
+                        lhsT=cq[:, P * a : P * a + P].bitcast(FP8X4),
+                        lhsT_scale=cs[:, P * a : P * a + P],
+                        rhs=wbq[:, 512 * part : 512 * part + 512].bitcast(FP8X4),
+                        rhs_scale=wbs[:, 512 * part : 512 * part + 512],
+                        start=True,
+                        stop=True,
+                    )
+                    banks.append(kv)
+            live["kv", q] = banks
+
+        with tc.tile_pool(name="outp", bufs=3) as outp:
+
+            def rotate(quad):
+                t0 = 4 * (quad % 2)
+                k_sb = outp.tile([P, 4, H, 256], F32, name="k_sb", tag="k_sb")
+                v_sb = outp.tile([P, 4, H * 128], F32, name="v_sb", tag="v_sb")
+                live["out", quad] = (k_sb, v_sb)
+                r_pairs = live["r", quad][:].rearrange("p t (j e) -> p t e j", e=2)
+                m1 = work.tile([P, 4, 2, 64], F32, name="m1", tag="m1", bufs=2)
+                nc.vector.tensor_tensor(
+                    out=m1[:],
+                    in0=r_pairs[:, :, 0:1, :].to_broadcast([P, 4, 2, 64]),
+                    in1=tab1[:, t0 : t0 + 4, :, :],
+                    op=ALU.mult,
+                )
+                m2 = work.tile([P, 4, 2, 64], F32, name="m2", tag="m2", bufs=2)
+                nc.vector.tensor_tensor(
+                    out=m2[:],
+                    in0=r_pairs[:, :, 1:2, :].to_broadcast([P, 4, 2, 64]),
+                    in1=tab2[:, t0 : t0 + 4, :, :],
+                    op=ALU.mult,
+                )
+                nc.gpsimd.tensor_tensor(
+                    out=k_sb[:, :, 0, 128:256].rearrange("p t (j e) -> p t j e", e=2),
+                    in0=m1[:].rearrange("p t e j -> p t j e"),
+                    in1=m2[:].rearrange("p t e j -> p t j e"),
+                    op=ALU.add,
+                )
+                nc.gpsimd.tensor_scalar(
+                    out=k_sb[:, :, 1:4, 128:256],
+                    in0=k_sb[:, :, 0:1, 128:256].to_broadcast([P, 4, 3, 128]),
+                    scalar1=1.0,
+                    scalar2=0.0,
+                    op0=ALU.mult,
+                    op1=ALU.add,
+                )
+
+            def copy_out(q):
+                k_sb, v_sb = live["out", q // 2]
+                for a in range(2):
+                    tt = 2 * (q % 2) + a
+                    eng = engines["SV"[a]]
+                    eng(out=k_sb[:, tt, :, 0:128], in_=live["kv", q][2 * a][:].rearrange("p (h d) -> p h d", h=H))
+                    eng(out=v_sb[:, tt, :], in_=live["kv", q][2 * a + 1][:])
+
+            def store(quad, lo, hi):
+                k_sb, v_sb = live["out", quad]
+                b = quad // 2
+                t0 = 4 * (quad % 2)
+                nc.sync.dma_start(
+                    out=k_rows[b][:, t0 + lo : t0 + hi, :], in_=k_sb[:, lo:hi].rearrange("p t h d -> p t (h d)")
+                )
+                nc.sync.dma_start(out=v_rows[b][:, t0 + lo : t0 + hi, :], in_=v_sb[:, lo:hi, :])
+
+            def is_pair(q):
+                return 0 <= q < N_PAIRS
+
+            x_transpose(0)
+            x_copy(0)
+            x_quantise(0)
+            next_x = 1
+            for n in range(N_PAIRS + 3):
+                fresh = [q for q in range(next_x, next_x + (2 if n < 3 else 1)) if is_pair(q)]
+                next_x = next_x + len(fresh)
+                for q in fresh:
+                    x_transpose(q)
+                if is_pair(n - 2):
+                    c_transpose(n - 2)
+                if is_pair(n - 1):
+                    squares(n - 1)
+                for q in fresh:
+                    x_copy(q)
+                if is_pair(n - 1):
+                    normalise(n - 1)
+                if is_pair(n - 2):
+                    c_copy(n - 2)
+                    c_quantise(n - 2)
+                for q in fresh:
+                    x_quantise(q)
+                if is_pair(n - 3):
+                    stage2(n - 3)
+                if n % 2 == 1 and n // 2 < N_QUADS:
+                    stage1_rotary(n // 2)
+                if is_pair(n):
+                    stage1_latent(n)
+                if n % 2 == 1 and n // 2 < N_QUADS:
+                    rotate(n // 2)
+                if is_pair(n - 3):
+                    q = n - 3
+                    copy_out(q)
+                    if q >= PAIR_STORES_FROM:
+                        store(q // 2, 2 * (q % 2), 2 * (q % 2) + 2)
+                    elif q % 2 == 1:
+                        store(q // 2, 0, 4)

@@ -17,10 +17,8 @@ B, T, C = 4, 1024, 1024
 KVL, R, H = 512, 128, 4
 TPP = 8
 N_PAIRS = B * TPP // 2
-N_QUADS = N_PAIRS // 2
 EPS = 1e-6
 RATIO = 10000.0 ** (-1.0 / 64.0)
-PAIR_STORES_FROM = 12
 
 FLOPS = 2 * B * T * C * (KVL + R) + 2 * B * T * KVL * (H * 256)
 
@@ -42,7 +40,6 @@ def tile_multiheadlatentattention_pb_t_kernel(tc, x, w_kva, kva_norm_w, w_kvb, o
         engines = {"S": nc.scalar.copy, "V": nc.vector.tensor_copy}
 
         g_bc = const.tile([P, KVL], BF16, name="g_bc")
-        nc.scalar.dma_start(out=g_bc[:], in_=kva_norm_w.partition_broadcast(P))
 
         waq = const.tile([P, 2 * 640], U32, name="waq", align_bytes=64)
         was = const.tile([P, 2 * 640], U8, name="was", align_bytes=64)
@@ -53,6 +50,11 @@ def tile_multiheadlatentattention_pb_t_kernel(tc, x, w_kva, kva_norm_w, w_kvb, o
         ident_f = const.tile([P, P], F32, name="ident_f")
         ident_b = const.tile([P, P], BF16, name="ident_b")
         eps_t = const.tile([P, 1], F32, name="eps_t")
+        sin_h = const.tile([P, TPP, 64], F32, name="sin_h")
+        sin_q = const.tile([P, TPP, 64], F32, name="sin_q")
+        sq_q = const.tile([P, TPP, 64], F32, name="sq_q")
+        cos_h = const.tile([P, TPP, 64], F32, name="cos_h")
+        sq_h = const.tile([P, TPP, 64], F32, name="sq_h")
 
         x_rows = x.rearrange("b (p t) k -> b p (t k)", t=TPP)
         k_rows = out_0.rearrange("b (p t) h d -> b p t (h d)", t=TPP)
@@ -75,6 +77,11 @@ def tile_multiheadlatentattention_pb_t_kernel(tc, x, w_kva, kva_norm_w, w_kvb, o
             )
 
         with tc.tile_pool(name="setup", bufs=1) as setup:
+            g_row = setup.tile([P, KVL], BF16, name="g_row")
+            nc.vector.memset(g_row[:], 0.0)
+            nc.scalar.dma_start(out=g_row[0:1, :], in_=kva_norm_w.rearrange("(o k) -> o k", o=1))
+            ones = setup.tile([P, P], BF16, name="ones")
+            nc.vector.memset(ones[:], 1.0)
             war = setup.tile([P, 5 * C], BF16, name="war")
             nc.sync.dma_start(
                 out=war[:].rearrange("p (r k) -> p r k", r=5), in_=w_kva.rearrange("(r p) k -> p r k", p=P)
@@ -117,32 +124,8 @@ def tile_multiheadlatentattention_pb_t_kernel(tc, x, w_kva, kva_norm_w, w_kvb, o
             nc.vector.tensor_copy(out=whole_f[:], in_=whole_i[:])
             frac = setup.tile([P, TPP, 64], F32, name="frac")
             nc.vector.tensor_tensor(out=frac[:], in0=turns[:], in1=whole_f[:], op=ALU.subtract)
-            sin_h = setup.tile([P, TPP, 64], F32, name="sin_h")
             nc.scalar.activation(out=sin_h[:], in_=frac[:], func=ACT.Sin, scale=math.pi)
-            sin_q = setup.tile([P, TPP, 64], F32, name="sin_q")
             nc.scalar.activation(out=sin_q[:], in_=frac[:], func=ACT.Sin, scale=0.5 * math.pi)
-            sq_q = setup.tile([P, TPP, 64], F32, name="sq_q")
-            nc.gpsimd.tensor_tensor(out=sq_q[:], in0=sin_q[:], in1=sin_q[:], op=ALU.mult)
-            cos_h = setup.tile([P, TPP, 64], F32, name="cos_h")
-            nc.gpsimd.tensor_scalar(
-                out=cos_h[:], in0=sq_q[:], scalar1=-2.0, scalar2=1.0, op0=ALU.mult, op1=ALU.add
-            )
-            prod = setup.tile([P, TPP, 64], F32, name="prod")
-            nc.gpsimd.tensor_tensor(out=prod[:], in0=sin_h[:], in1=cos_h[:], op=ALU.mult)
-            nc.gpsimd.tensor_scalar(
-                out=tab1[:, :, 1, :], in0=prod[:], scalar1=2.0, scalar2=0.0, op0=ALU.mult, op1=ALU.add
-            )
-            nc.gpsimd.tensor_scalar(
-                out=tab2[:, :, 0, :], in0=prod[:], scalar1=-2.0, scalar2=0.0, op0=ALU.mult, op1=ALU.add
-            )
-            sq_h = setup.tile([P, TPP, 64], F32, name="sq_h")
-            nc.gpsimd.tensor_tensor(out=sq_h[:], in0=sin_h[:], in1=sin_h[:], op=ALU.mult)
-            nc.gpsimd.tensor_scalar(
-                out=tab1[:, :, 0, :], in0=sq_h[:], scalar1=-2.0, scalar2=1.0, op0=ALU.mult, op1=ALU.add
-            )
-            nc.gpsimd.tensor_scalar(
-                out=tab2[:, :, 1, :], in0=sq_h[:], scalar1=-2.0, scalar2=1.0, op0=ALU.mult, op1=ALU.add
-            )
 
             war_w = war[:].bitcast(F32)
             for r in range(5):
@@ -171,6 +154,23 @@ def tile_multiheadlatentattention_pb_t_kernel(tc, x, w_kva, kva_norm_w, w_kvb, o
                 nc.vector.quantize_mx(
                     out=wbq[:, dest : dest + 256].bitcast(FP8X4), scales=wbs[:, dest : dest + 256], in_=grp[:]
                 )
+
+            g_ps = k_bank([P, KVL], F32, "g_ps")
+            nc.tensor.matmul(out=g_ps[:], lhsT=ones[:], rhs=g_row[:], start=True, stop=True)
+            nc.scalar.copy(out=g_bc[:], in_=g_ps[:])
+
+        def finish_tables():
+            nc.scalar.activation(out=sq_q[:], in_=sin_q[:], func=ACT.Square)
+            nc.scalar.activation(out=cos_h[:], in_=sq_q[:], func=ACT.Copy, scale=-2.0, bias=1.0)
+            nc.scalar.activation(out=sq_h[:], in_=sin_h[:], func=ACT.Square)
+            nc.scalar.activation(out=tab1[:, :, 0, :], in_=sq_h[:], func=ACT.Copy, scale=-2.0, bias=1.0)
+            nc.scalar.activation(out=tab2[:, :, 1, :], in_=sq_h[:], func=ACT.Copy, scale=-2.0, bias=1.0)
+            nc.vector.scalar_tensor_tensor(
+                out=tab1[:, :, 1, :], in0=sin_h[:], scalar=2.0, in1=cos_h[:], op0=ALU.mult, op1=ALU.mult
+            )
+            nc.vector.scalar_tensor_tensor(
+                out=tab2[:, :, 0, :], in0=sin_h[:], scalar=-2.0, in1=cos_h[:], op0=ALU.mult, op1=ALU.mult
+            )
 
         def x_transpose(q):
             live["xt", q] = [
@@ -212,12 +212,12 @@ def tile_multiheadlatentattention_pb_t_kernel(tc, x, w_kva, kva_norm_w, w_kvb, o
                 tiles.append(l)
             live["l", q] = tiles
 
-        def stage1_rotary(quad):
-            r_ps = psum.tile([P, 4, R], F32, name="r_ps", tag="R")
-            for tt in range(4):
+        def stage1_rotary(q):
+            r_ps = psum.tile([P, 2, R], F32, name="r_ps", tag="R")
+            for a in range(2):
                 for g in range(2):
-                    stage1_pass(r_ps[:, tt, :], 2 * quad + tt // 2, tt % 2, g, KVL, KVL + R)
-            live["r", quad] = r_ps
+                    stage1_pass(r_ps[:, a, :], q, a, g, KVL, KVL + R)
+            live["r", q] = r_ps
 
         def squares(q):
             ssq = small.tile([P, 2], F32, name="ssq", tag="ssq")
@@ -284,26 +284,26 @@ def tile_multiheadlatentattention_pb_t_kernel(tc, x, w_kva, kva_norm_w, w_kvb, o
                     banks.append(kv)
             live["kv", q] = banks
 
-        with tc.tile_pool(name="outp", bufs=3) as outp:
+        with tc.tile_pool(name="outp", bufs=6) as outp:
 
-            def rotate(quad):
-                t0 = 4 * (quad % 2)
-                k_sb = outp.tile([P, 4, H, 256], F32, name="k_sb", tag="k_sb")
-                v_sb = outp.tile([P, 4, H * 128], F32, name="v_sb", tag="v_sb")
-                live["out", quad] = (k_sb, v_sb)
-                r_pairs = live["r", quad][:].rearrange("p t (j e) -> p t e j", e=2)
-                m1 = work.tile([P, 4, 2, 64], F32, name="m1", tag="m1", bufs=2)
+            def rotate(q):
+                t0 = 2 * (q % 4)
+                k_sb = outp.tile([P, 2, H, 256], F32, name="k_sb", tag="k_sb")
+                v_sb = outp.tile([P, 2, H * 128], F32, name="v_sb", tag="v_sb")
+                live["out", q] = (k_sb, v_sb)
+                r_pairs = live["r", q][:].rearrange("p t (j e) -> p t e j", e=2)
+                m1 = work.tile([P, 2, 2, 64], F32, name="m1", tag="m1")
                 nc.vector.tensor_tensor(
                     out=m1[:],
-                    in0=r_pairs[:, :, 0:1, :].to_broadcast([P, 4, 2, 64]),
-                    in1=tab1[:, t0 : t0 + 4, :, :],
+                    in0=r_pairs[:, :, 0:1, :].to_broadcast([P, 2, 2, 64]),
+                    in1=tab1[:, t0 : t0 + 2, :, :],
                     op=ALU.mult,
                 )
-                m2 = work.tile([P, 4, 2, 64], F32, name="m2", tag="m2", bufs=2)
+                m2 = work.tile([P, 2, 2, 64], F32, name="m2", tag="m2")
                 nc.vector.tensor_tensor(
                     out=m2[:],
-                    in0=r_pairs[:, :, 1:2, :].to_broadcast([P, 4, 2, 64]),
-                    in1=tab2[:, t0 : t0 + 4, :, :],
+                    in0=r_pairs[:, :, 1:2, :].to_broadcast([P, 2, 2, 64]),
+                    in1=tab2[:, t0 : t0 + 2, :, :],
                     op=ALU.mult,
                 )
                 nc.gpsimd.tensor_tensor(
@@ -314,7 +314,7 @@ def tile_multiheadlatentattention_pb_t_kernel(tc, x, w_kva, kva_norm_w, w_kvb, o
                 )
                 nc.gpsimd.tensor_scalar(
                     out=k_sb[:, :, 1:4, 128:256],
-                    in0=k_sb[:, :, 0:1, 128:256].to_broadcast([P, 4, 3, 128]),
+                    in0=k_sb[:, :, 0:1, 128:256].to_broadcast([P, 2, 3, 128]),
                     scalar1=1.0,
                     scalar2=0.0,
                     op0=ALU.mult,
@@ -322,21 +322,18 @@ def tile_multiheadlatentattention_pb_t_kernel(tc, x, w_kva, kva_norm_w, w_kvb, o
                 )
 
             def copy_out(q):
-                k_sb, v_sb = live["out", q // 2]
+                k_sb, v_sb = live["out", q]
                 for a in range(2):
-                    tt = 2 * (q % 2) + a
                     eng = engines["SV"[a]]
-                    eng(out=k_sb[:, tt, :, 0:128], in_=live["kv", q][2 * a][:].rearrange("p (h d) -> p h d", h=H))
-                    eng(out=v_sb[:, tt, :], in_=live["kv", q][2 * a + 1][:])
+                    eng(out=k_sb[:, a, :, 0:128], in_=live["kv", q][2 * a][:].rearrange("p (h d) -> p h d", h=H))
+                    eng(out=v_sb[:, a, :], in_=live["kv", q][2 * a + 1][:])
 
-            def store(quad, lo, hi):
-                k_sb, v_sb = live["out", quad]
-                b = quad // 2
-                t0 = 4 * (quad % 2)
-                nc.sync.dma_start(
-                    out=k_rows[b][:, t0 + lo : t0 + hi, :], in_=k_sb[:, lo:hi].rearrange("p t h d -> p t (h d)")
-                )
-                nc.sync.dma_start(out=v_rows[b][:, t0 + lo : t0 + hi, :], in_=v_sb[:, lo:hi, :])
+            def store(q):
+                k_sb, v_sb = live["out", q]
+                b = q // 4
+                t0 = 2 * (q % 4)
+                nc.sync.dma_start(out=k_rows[b][:, t0 : t0 + 2, :], in_=k_sb[:].rearrange("p t h d -> p t (h d)"))
+                nc.sync.dma_start(out=v_rows[b][:, t0 : t0 + 2, :], in_=v_sb[:])
 
             def is_pair(q):
                 return 0 <= q < N_PAIRS
@@ -363,18 +360,16 @@ def tile_multiheadlatentattention_pb_t_kernel(tc, x, w_kva, kva_norm_w, w_kvb, o
                     c_quantise(n - 2)
                 for q in fresh:
                     x_quantise(q)
+                if n == 0:
+                    finish_tables()
                 if is_pair(n - 3):
                     stage2(n - 3)
-                if n % 2 == 1 and n // 2 < N_QUADS:
-                    stage1_rotary(n // 2)
+                if is_pair(n - 1):
+                    stage1_rotary(n - 1)
                 if is_pair(n):
                     stage1_latent(n)
-                if n % 2 == 1 and n // 2 < N_QUADS:
-                    rotate(n // 2)
+                if is_pair(n - 1):
+                    rotate(n - 1)
                 if is_pair(n - 3):
-                    q = n - 3
-                    copy_out(q)
-                    if q >= PAIR_STORES_FROM:
-                        store(q // 2, 2 * (q % 2), 2 * (q % 2) + 2)
-                    elif q % 2 == 1:
-                        store(q // 2, 0, 4)
+                    copy_out(n - 3)
+                    store(n - 3)

@@ -76,30 +76,49 @@ def tile_multiheadlatentattention_pb_t_kernel(tc, x, w_kva, kva_norm_w, w_kvb, o
                 in_=xt[:].rearrange("p (g u w) -> p g w u", g=2, u=2),
             )
 
-        with tc.tile_pool(name="setup", bufs=1) as setup:
-            g_row = setup.tile([P, KVL], BF16, name="g_row")
-            nc.vector.memset(g_row[:], 0.0)
-            nc.scalar.dma_start(out=g_row[0:1, :], in_=kva_norm_w.rearrange("(o k) -> o k", o=1))
-            ones = setup.tile([P, P], BF16, name="ones")
-            nc.vector.memset(ones[:], 1.0)
-            war = setup.tile([P, 5 * C], BF16, name="war")
-            nc.sync.dma_start(
-                out=war[:].rearrange("p (r k) -> p r k", r=5), in_=w_kva.rearrange("(r p) k -> p r k", p=P)
-            )
-            wbr = setup.tile([P, 8 * KVL], BF16, name="wbr")
-            nc.sync.dma_start(
-                out=wbr[:].rearrange("p (r k) -> p r k", r=8), in_=w_kvb.rearrange("(r p) k -> p r k", p=P)
-            )
-            for hb in range(8):
-                xr = xin.tile([P, 4 * C], BF16, name="xr", tag="xr")
-                nc.sync.dma_start(out=xr[:], in_=x_rows[hb // 2][:, 4 * C * (hb % 2) : 4 * C * (hb % 2) + 4 * C])
-                x_words.append(xr[:].bitcast(F32))
+        g_row = const.tile([P, KVL], BF16, name="g_row")
+        nc.vector.memset(g_row[:], 0.0)
+        ones = const.tile([P, P], BF16, name="ones")
+        nc.vector.memset(ones[:], 1.0)
+        nc.vector.memset(eps_t[:], EPS)
+        wa_rows = w_kva.rearrange("(r p) k -> p r k", p=P)
+        war = xin.tile([P, 4 * C], BF16, name="war", tag="xr")
+        war_r = const.tile([P, C], BF16, name="war_r")
+        wbr = None
 
+        def load_x(hb):
+            xr = xin.tile([P, 4 * C], BF16, name="xr", tag="xr")
+            x_words.append(xr[:].bitcast(F32))
+            nc.sync.dma_start(out=xr[:], in_=x_rows[hb // 2][:, 4 * C * (hb % 2) : 4 * C * (hb % 2) + 4 * C])
+
+        for step in range(9):
+            if step < 2:
+                nc.sync.dma_start(
+                    out=war[:, 2 * C * step : 2 * C * step + 2 * C].rearrange("p (r k) -> p r k", r=2),
+                    in_=wa_rows[:, 2 * step : 2 * step + 2, :],
+                )
+            elif step == 2:
+                xr = xin.tile([P, 4 * C], BF16, name="xr", tag="xr")
+                x_words.append(xr[:].bitcast(F32))
+                nc.sync.dma_start(out=xr[:, 0 : 2 * C], in_=x_rows[0][:, 0 : 2 * C])
+                nc.sync.dma_start(out=war_r[:], in_=wa_rows[:, 4, :])
+                nc.sync.dma_start(out=g_row[0:1, :], in_=kva_norm_w.rearrange("(o k) -> o k", o=1))
+                nc.sync.dma_start(out=xr[:, 2 * C : 4 * C], in_=x_rows[0][:, 2 * C : 4 * C])
+            elif step == 3:
+                wbr = xin.tile([P, 8 * KVL], BF16, name="wbr", tag="xr")
+                nc.sync.dma_start(
+                    out=wbr[:].rearrange("p (r k) -> p r k", r=8), in_=w_kvb.rearrange("(r p) k -> p r k", p=P)
+                )
+            elif step < 9:
+                load_x(step - 3)
+
+        warm = const.tile([P, 2], F32, name="warm")
+        nc.scalar.activation(out=warm[:, 0:1], in_=eps_t[:], func=ACT.Sin)
+        with tc.tile_pool(name="setup", bufs=1) as setup:
             pos_i = setup.tile([P, TPP], I32, name="pos_i")
             nc.gpsimd.iota(pos_i[:], pattern=[[1, TPP]], base=0, channel_multiplier=TPP)
             make_identity(nc, ident_f[:])
             make_identity(nc, ident_b[:])
-            nc.vector.memset(eps_t[:], EPS)
             pos_f = setup.tile([P, TPP], F32, name="pos_f")
             nc.vector.tensor_copy(out=pos_f[:], in_=pos_i[:])
             inv = setup.tile([P, 64], F32, name="inv")
@@ -127,34 +146,33 @@ def tile_multiheadlatentattention_pb_t_kernel(tc, x, w_kva, kva_norm_w, w_kvb, o
             nc.scalar.activation(out=sin_h[:], in_=frac[:], func=ACT.Sin, scale=math.pi)
             nc.scalar.activation(out=sin_q[:], in_=frac[:], func=ACT.Sin, scale=0.5 * math.pi)
 
-            war_w = war[:].bitcast(F32)
-            for r in range(5):
-                xt = transpose_words(war_w[:, 512 * r : 512 * r + 512])
-                grp = stage.tile([P, 1024], BF16, name="grp", tag="cgrp", align_bytes=64)
-                copy_words(xt, grp[:], "SV"[r % 2])
-                for g in range(2):
-                    cols = slice(640 * g + P * r, 640 * g + P * r + P)
-                    nc.vector.quantize_mx(
-                        out=waq[:, cols].bitcast(FP8X4), scales=was[:, cols], in_=grp[:, 512 * g : 512 * g + 512]
-                    )
-            for n, (ra, rb, dest) in enumerate(((0, 2, 0), (4, 6, 256), (1, 3, 512), (5, 7, 768))):
-                wt = k_bank([P, 2, 4, P], BF16, "wt")
-                for a, r in enumerate((ra, rb)):
-                    for j in range(4):
-                        nc.tensor.transpose(
-                            out=wt[:, a, j, :],
-                            in_=wbr[:, KVL * r + P * j : KVL * r + P * j + P],
-                            identity=ident_b[:],
-                        )
-                grp = stage.tile([P, 1024], BF16, name="grp", tag="cgrp", align_bytes=64)
-                engines["VS"[n % 2]](
-                    out=grp[:].rearrange("p (a w j) -> p a w j", a=2, j=4),
-                    in_=wt[:].rearrange("p a j w -> p a w j"),
-                )
+        def prepare_wa(r, eng):
+            src = war_r[:].bitcast(F32) if r == 4 else war[:].bitcast(F32)[:, 512 * r : 512 * r + 512]
+            xt = transpose_words(src)
+            grp = stage.tile([P, 1024], BF16, name="grp", tag="cgrp", align_bytes=64)
+            copy_words(xt, grp[:], eng)
+            for g in range(2):
+                cols = slice(640 * g + P * r, 640 * g + P * r + P)
                 nc.vector.quantize_mx(
-                    out=wbq[:, dest : dest + 256].bitcast(FP8X4), scales=wbs[:, dest : dest + 256], in_=grp[:]
+                    out=waq[:, cols].bitcast(FP8X4), scales=was[:, cols], in_=grp[:, 512 * g : 512 * g + 512]
                 )
 
+        def prepare_wb(ra, rb, dest, eng):
+            wt = k_bank([P, 2, 4, P], BF16, "wt")
+            for a, r in enumerate((ra, rb)):
+                for j in range(4):
+                    nc.tensor.transpose(
+                        out=wt[:, a, j, :], in_=wbr[:, KVL * r + P * j : KVL * r + P * j + P], identity=ident_b[:]
+                    )
+            grp = stage.tile([P, 1024], BF16, name="grp", tag="cgrp", align_bytes=64)
+            engines[eng](
+                out=grp[:].rearrange("p (a w j) -> p a w j", a=2, j=4), in_=wt[:].rearrange("p a j w -> p a w j")
+            )
+            nc.vector.quantize_mx(
+                out=wbq[:, dest : dest + 256].bitcast(FP8X4), scales=wbs[:, dest : dest + 256], in_=grp[:]
+            )
+
+        def spread_gain():
             g_ps = k_bank([P, KVL], F32, "g_ps")
             nc.tensor.matmul(out=g_ps[:], lhsT=ones[:], rhs=g_row[:], start=True, stop=True)
             nc.scalar.copy(out=g_bc[:], in_=g_ps[:])
@@ -171,6 +189,7 @@ def tile_multiheadlatentattention_pb_t_kernel(tc, x, w_kva, kva_norm_w, w_kvb, o
             nc.vector.scalar_tensor_tensor(
                 out=tab2[:, :, 0, :], in0=sin_h[:], scalar=-2.0, in1=cos_h[:], op0=ALU.mult, op1=ALU.mult
             )
+            nc.scalar.activation(out=warm[:, 1:2], in_=eps_t[:], func=ACT.Abs_reciprocal_sqrt)
 
         def x_transpose(q):
             live["xt", q] = [
@@ -224,13 +243,14 @@ def tile_multiheadlatentattention_pb_t_kernel(tc, x, w_kva, kva_norm_w, w_kvb, o
             for a in range(2):
                 junk = work.tile([P, KVL], BF16, name="junk", tag="junk", bufs=2)
                 nc.scalar.activation(out=junk[:], in_=live["l", q][a][:], func=ACT.Square, accum_out=ssq[:, a : a + 1])
-            std = small.tile([P, 2], F32, name="std", tag="std")
-            nc.scalar.activation(out=std[:], in_=ssq[:], func=ACT.Sqrt, scale=1.0 / KVL, bias=eps_t[:, 0:1])
-            live["std", q] = std
+            rstd = small.tile([P, 2], F32, name="rstd", tag="rstd")
+            nc.scalar.activation(
+                out=rstd[:], in_=ssq[:], func=ACT.Abs_reciprocal_sqrt, scale=1.0 / KVL, bias=eps_t[:, 0:1]
+            )
+            live["rstd", q] = rstd
 
         def normalise(q):
-            rstd = small.tile([P, 2], F32, name="rstd", tag="rstd")
-            nc.vector.reciprocal(out=rstd[:], in_=live["std", q][:])
+            rstd = live["rstd", q]
             c_sb = work.tile([P, 2, KVL], BF16, name="c_sb", tag="c_sb")
             for a in range(2):
                 nc.vector.scalar_tensor_tensor(
@@ -338,15 +358,18 @@ def tile_multiheadlatentattention_pb_t_kernel(tc, x, w_kva, kva_norm_w, w_kvb, o
             def is_pair(q):
                 return 0 <= q < N_PAIRS
 
+            for r in range(4):
+                prepare_wa(r, "SV"[r % 2])
+            load_x(6)
             x_transpose(0)
             x_copy(0)
             x_quantise(0)
-            next_x = 1
             for n in range(N_PAIRS + 3):
-                fresh = [q for q in range(next_x, next_x + (2 if n < 3 else 1)) if is_pair(q)]
-                next_x = next_x + len(fresh)
+                fresh = [q for q in (n + 1,) if is_pair(q)]
                 for q in fresh:
                     x_transpose(q)
+                if n == 0:
+                    load_x(7)
                 if is_pair(n - 2):
                     c_transpose(n - 2)
                 if is_pair(n - 1):
@@ -360,8 +383,6 @@ def tile_multiheadlatentattention_pb_t_kernel(tc, x, w_kva, kva_norm_w, w_kvb, o
                     c_quantise(n - 2)
                 for q in fresh:
                     x_quantise(q)
-                if n == 0:
-                    finish_tables()
                 if is_pair(n - 3):
                     stage2(n - 3)
                 if is_pair(n - 1):
@@ -373,3 +394,12 @@ def tile_multiheadlatentattention_pb_t_kernel(tc, x, w_kva, kva_norm_w, w_kvb, o
                 if is_pair(n - 3):
                     copy_out(n - 3)
                     store(n - 3)
+                if n == 0:
+                    prepare_wa(4, "S")
+                    spread_gain()
+                    finish_tables()
+                    prepare_wb(0, 2, 0, "V")
+                    prepare_wb(4, 6, 256, "S")
+                if n == 1:
+                    prepare_wb(1, 3, 512, "V")
+                    prepare_wb(5, 7, 768, "S")

@@ -332,13 +332,11 @@ def tile_multiheadlatentattention_pb_t_kernel(tc, x, w_kva, kva_norm_w, w_kvb, o
                     in1=m2[:].rearrange("p t e j -> p t j e"),
                     op=ALU.add,
                 )
-                nc.gpsimd.tensor_scalar(
-                    out=k_sb[:, :, 1:4, 128:256],
-                    in0=k_sb[:, :, 0:1, 128:256].to_broadcast([P, 2, 3, 128]),
-                    scalar1=1.0,
-                    scalar2=0.0,
-                    op0=ALU.mult,
-                    op1=ALU.add,
+
+            def share_rotary(q):
+                k_sb = live["out", q][0]
+                nc.vector.tensor_copy(
+                    out=k_sb[:, :, 1:4, 128:256], in_=k_sb[:, :, 0:1, 128:256].to_broadcast([P, 2, 3, 128])
                 )
 
             def copy_out(q):
@@ -389,6 +387,8 @@ def tile_multiheadlatentattention_pb_t_kernel(tc, x, w_kva, kva_norm_w, w_kvb, o
                     stage1_rotary(n - 1)
                 if is_pair(n):
                     stage1_latent(n)
+                if is_pair(n - 2):
+                    share_rotary(n - 2)
                 if is_pair(n - 1):
                     rotate(n - 1)
                 if is_pair(n - 3):

@@ -76,49 +76,30 @@ def tile_multiheadlatentattention_pb_t_kernel(tc, x, w_kva, kva_norm_w, w_kvb, o
                 in_=xt[:].rearrange("p (g u w) -> p g w u", g=2, u=2),
             )
 
-        g_row = const.tile([P, KVL], BF16, name="g_row")
-        nc.vector.memset(g_row[:], 0.0)
-        ones = const.tile([P, P], BF16, name="ones")
-        nc.vector.memset(ones[:], 1.0)
-        nc.vector.memset(eps_t[:], EPS)
-        wa_rows = w_kva.rearrange("(r p) k -> p r k", p=P)
-        war = xin.tile([P, 4 * C], BF16, name="war", tag="xr")
-        war_r = const.tile([P, C], BF16, name="war_r")
-        wbr = None
-
-        def load_x(hb):
-            xr = xin.tile([P, 4 * C], BF16, name="xr", tag="xr")
-            x_words.append(xr[:].bitcast(F32))
-            nc.sync.dma_start(out=xr[:], in_=x_rows[hb // 2][:, 4 * C * (hb % 2) : 4 * C * (hb % 2) + 4 * C])
-
-        for step in range(9):
-            if step < 2:
-                nc.sync.dma_start(
-                    out=war[:, 2 * C * step : 2 * C * step + 2 * C].rearrange("p (r k) -> p r k", r=2),
-                    in_=wa_rows[:, 2 * step : 2 * step + 2, :],
-                )
-            elif step == 2:
-                xr = xin.tile([P, 4 * C], BF16, name="xr", tag="xr")
-                x_words.append(xr[:].bitcast(F32))
-                nc.sync.dma_start(out=xr[:, 0 : 2 * C], in_=x_rows[0][:, 0 : 2 * C])
-                nc.sync.dma_start(out=war_r[:], in_=wa_rows[:, 4, :])
-                nc.sync.dma_start(out=g_row[0:1, :], in_=kva_norm_w.rearrange("(o k) -> o k", o=1))
-                nc.sync.dma_start(out=xr[:, 2 * C : 4 * C], in_=x_rows[0][:, 2 * C : 4 * C])
-            elif step == 3:
-                wbr = xin.tile([P, 8 * KVL], BF16, name="wbr", tag="xr")
-                nc.sync.dma_start(
-                    out=wbr[:].rearrange("p (r k) -> p r k", r=8), in_=w_kvb.rearrange("(r p) k -> p r k", p=P)
-                )
-            elif step < 9:
-                load_x(step - 3)
-
-        warm = const.tile([P, 2], F32, name="warm")
-        nc.scalar.activation(out=warm[:, 0:1], in_=eps_t[:], func=ACT.Sin)
         with tc.tile_pool(name="setup", bufs=1) as setup:
+            g_row = setup.tile([P, KVL], BF16, name="g_row")
+            nc.vector.memset(g_row[:], 0.0)
+            nc.scalar.dma_start(out=g_row[0:1, :], in_=kva_norm_w.rearrange("(o k) -> o k", o=1))
+            ones = setup.tile([P, P], BF16, name="ones")
+            nc.vector.memset(ones[:], 1.0)
+            war = setup.tile([P, 5 * C], BF16, name="war")
+            nc.sync.dma_start(
+                out=war[:].rearrange("p (r k) -> p r k", r=5), in_=w_kva.rearrange("(r p) k -> p r k", p=P)
+            )
+            wbr = setup.tile([P, 8 * KVL], BF16, name="wbr")
+            nc.sync.dma_start(
+                out=wbr[:].rearrange("p (r k) -> p r k", r=8), in_=w_kvb.rearrange("(r p) k -> p r k", p=P)
+            )
+            for hb in range(8):
+                xr = xin.tile([P, 4 * C], BF16, name="xr", tag="xr")
+                nc.sync.dma_start(out=xr[:], in_=x_rows[hb // 2][:, 4 * C * (hb % 2) : 4 * C * (hb % 2) + 4 * C])
+                x_words.append(xr[:].bitcast(F32))
+
             pos_i = setup.tile([P, TPP], I32, name="pos_i")
             nc.gpsimd.iota(pos_i[:], pattern=[[1, TPP]], base=0, channel_multiplier=TPP)
             make_identity(nc, ident_f[:])
             make_identity(nc, ident_b[:])
+            nc.vector.memset(eps_t[:], EPS)
             pos_f = setup.tile([P, TPP], F32, name="pos_f")
             nc.vector.tensor_copy(out=pos_f[:], in_=pos_i[:])
             inv = setup.tile([P, 64], F32, name="inv")
@@ -146,33 +127,34 @@ def tile_multiheadlatentattention_pb_t_kernel(tc, x, w_kva, kva_norm_w, w_kvb, o
             nc.scalar.activation(out=sin_h[:], in_=frac[:], func=ACT.Sin, scale=math.pi)
             nc.scalar.activation(out=sin_q[:], in_=frac[:], func=ACT.Sin, scale=0.5 * math.pi)
 
-        def prepare_wa(r, eng):
-            src = war_r[:].bitcast(F32) if r == 4 else war[:].bitcast(F32)[:, 512 * r : 512 * r + 512]
-            xt = transpose_words(src)
-            grp = stage.tile([P, 1024], BF16, name="grp", tag="cgrp", align_bytes=64)
-            copy_words(xt, grp[:], eng)
-            for g in range(2):
-                cols = slice(640 * g + P * r, 640 * g + P * r + P)
+            war_w = war[:].bitcast(F32)
+            for r in range(5):
+                xt = transpose_words(war_w[:, 512 * r : 512 * r + 512])
+                grp = stage.tile([P, 1024], BF16, name="grp", tag="cgrp", align_bytes=64)
+                copy_words(xt, grp[:], "SV"[r % 2])
+                for g in range(2):
+                    cols = slice(640 * g + P * r, 640 * g + P * r + P)
+                    nc.vector.quantize_mx(
+                        out=waq[:, cols].bitcast(FP8X4), scales=was[:, cols], in_=grp[:, 512 * g : 512 * g + 512]
+                    )
+            for n, (ra, rb, dest) in enumerate(((0, 2, 0), (4, 6, 256), (1, 3, 512), (5, 7, 768))):
+                wt = k_bank([P, 2, 4, P], BF16, "wt")
+                for a, r in enumerate((ra, rb)):
+                    for j in range(4):
+                        nc.tensor.transpose(
+                            out=wt[:, a, j, :],
+                            in_=wbr[:, KVL * r + P * j : KVL * r + P * j + P],
+                            identity=ident_b[:],
+                        )
+                grp = stage.tile([P, 1024], BF16, name="grp", tag="cgrp", align_bytes=64)
+                engines["VS"[n % 2]](
+                    out=grp[:].rearrange("p (a w j) -> p a w j", a=2, j=4),
+                    in_=wt[:].rearrange("p a j w -> p a w j"),
+                )
                 nc.vector.quantize_mx(
-                    out=waq[:, cols].bitcast(FP8X4), scales=was[:, cols], in_=grp[:, 512 * g : 512 * g + 512]
+                    out=wbq[:, dest : dest + 256].bitcast(FP8X4), scales=wbs[:, dest : dest + 256], in_=grp[:]
                 )
 
-        def prepare_wb(ra, rb, dest, eng):
-            wt = k_bank([P, 2, 4, P], BF16, "wt")
-            for a, r in enumerate((ra, rb)):
-                for j in range(4):
-                    nc.tensor.transpose(
-                        out=wt[:, a, j, :], in_=wbr[:, KVL * r + P * j : KVL * r + P * j + P], identity=ident_b[:]
-                    )
-            grp = stage.tile([P, 1024], BF16, name="grp", tag="cgrp", align_bytes=64)
-            engines[eng](
-                out=grp[:].rearrange("p (a w j) -> p a w j", a=2, j=4), in_=wt[:].rearrange("p a j w -> p a w j")
-            )
-            nc.vector.quantize_mx(
-                out=wbq[:, dest : dest + 256].bitcast(FP8X4), scales=wbs[:, dest : dest + 256], in_=grp[:]
-            )
-
-        def spread_gain():
             g_ps = k_bank([P, KVL], F32, "g_ps")
             nc.tensor.matmul(out=g_ps[:], lhsT=ones[:], rhs=g_row[:], start=True, stop=True)
             nc.scalar.copy(out=g_bc[:], in_=g_ps[:])
@@ -189,7 +171,6 @@ def tile_multiheadlatentattention_pb_t_kernel(tc, x, w_kva, kva_norm_w, w_kvb, o
             nc.vector.scalar_tensor_tensor(
                 out=tab2[:, :, 0, :], in0=sin_h[:], scalar=-2.0, in1=cos_h[:], op0=ALU.mult, op1=ALU.mult
             )
-            nc.scalar.activation(out=warm[:, 1:2], in_=eps_t[:], func=ACT.Abs_reciprocal_sqrt)
 
         def x_transpose(q):
             live["xt", q] = [
@@ -332,11 +313,13 @@ def tile_multiheadlatentattention_pb_t_kernel(tc, x, w_kva, kva_norm_w, w_kvb, o
                     in1=m2[:].rearrange("p t e j -> p t j e"),
                     op=ALU.add,
                 )
-
-            def share_rotary(q):
-                k_sb = live["out", q][0]
-                nc.vector.tensor_copy(
-                    out=k_sb[:, :, 1:4, 128:256], in_=k_sb[:, :, 0:1, 128:256].to_broadcast([P, 2, 3, 128])
+                nc.gpsimd.tensor_scalar(
+                    out=k_sb[:, :, 1:4, 128:256],
+                    in0=k_sb[:, :, 0:1, 128:256].to_broadcast([P, 2, 3, 128]),
+                    scalar1=1.0,
+                    scalar2=0.0,
+                    op0=ALU.mult,
+                    op1=ALU.add,
                 )
 
             def copy_out(q):
@@ -356,18 +339,15 @@ def tile_multiheadlatentattention_pb_t_kernel(tc, x, w_kva, kva_norm_w, w_kvb, o
             def is_pair(q):
                 return 0 <= q < N_PAIRS
 
-            for r in range(4):
-                prepare_wa(r, "SV"[r % 2])
-            load_x(6)
             x_transpose(0)
             x_copy(0)
             x_quantise(0)
+            next_x = 1
             for n in range(N_PAIRS + 3):
-                fresh = [q for q in (n + 1,) if is_pair(q)]
+                fresh = [q for q in range(next_x, next_x + (2 if n < 3 else 1)) if is_pair(q)]
+                next_x = next_x + len(fresh)
                 for q in fresh:
                     x_transpose(q)
-                if n == 0:
-                    load_x(7)
                 if is_pair(n - 2):
                     c_transpose(n - 2)
                 if is_pair(n - 1):
@@ -381,25 +361,16 @@ def tile_multiheadlatentattention_pb_t_kernel(tc, x, w_kva, kva_norm_w, w_kvb, o
                     c_quantise(n - 2)
                 for q in fresh:
                     x_quantise(q)
+                if n == 0:
+                    finish_tables()
                 if is_pair(n - 3):
                     stage2(n - 3)
                 if is_pair(n - 1):
                     stage1_rotary(n - 1)
                 if is_pair(n):
                     stage1_latent(n)
-                if is_pair(n - 2):
-                    share_rotary(n - 2)
                 if is_pair(n - 1):
                     rotate(n - 1)
                 if is_pair(n - 3):
                     copy_out(n - 3)
                     store(n - 3)
-                if n == 0:
-                    prepare_wa(4, "S")
-                    spread_gain()
-                    finish_tables()
-                    prepare_wb(0, 2, 0, "V")
-                    prepare_wb(4, 6, 256, "S")
-                if n == 1:
-                    prepare_wb(1, 3, 512, "V")
-                    prepare_wb(5, 7, 768, "S")

@@ -221,13 +221,17 @@ def tile_multiheadlatentattention_pb_t_kernel(tc, x, w_kva, kva_norm_w, w_kvb, o
 
         def squares(q):
             ssq = small.tile([P, 2], F32, name="ssq", tag="ssq")
+            rstd = small.tile([P, 2], F32, name="rstd", tag="rstd")
             for a in range(2):
                 junk = work.tile([P, KVL], BF16, name="junk", tag="junk", bufs=2)
                 nc.scalar.activation(out=junk[:], in_=live["l", q][a][:], func=ACT.Square, accum_out=ssq[:, a : a + 1])
-            rstd = small.tile([P, 2], F32, name="rstd", tag="rstd")
-            nc.scalar.activation(
-                out=rstd[:], in_=ssq[:], func=ACT.Abs_reciprocal_sqrt, scale=1.0 / KVL, bias=eps_t[:, 0:1]
-            )
+                nc.scalar.activation(
+                    out=rstd[:, a : a + 1],
+                    in_=ssq[:, a : a + 1],
+                    func=ACT.Abs_reciprocal_sqrt,
+                    scale=1.0 / KVL,
+                    bias=eps_t[:, 0:1],
+                )
             live["rstd", q] = rstd
 
         def normalise(q):

@@ -221,17 +221,13 @@ def tile_multiheadlatentattention_pb_t_kernel(tc, x, w_kva, kva_norm_w, w_kvb, o
 
         def squares(q):
             ssq = small.tile([P, 2], F32, name="ssq", tag="ssq")
-            rstd = small.tile([P, 2], F32, name="rstd", tag="rstd")
             for a in range(2):
                 junk = work.tile([P, KVL], BF16, name="junk", tag="junk", bufs=2)
                 nc.scalar.activation(out=junk[:], in_=live["l", q][a][:], func=ACT.Square, accum_out=ssq[:, a : a + 1])
-                nc.scalar.activation(
-                    out=rstd[:, a : a + 1],
-                    in_=ssq[:, a : a + 1],
-                    func=ACT.Abs_reciprocal_sqrt,
-                    scale=1.0 / KVL,
-                    bias=eps_t[:, 0:1],
-                )
+            rstd = small.tile([P, 2], F32, name="rstd", tag="rstd")
+            nc.scalar.activation(
+                out=rstd[:], in_=ssq[:], func=ACT.Abs_reciprocal_sqrt, scale=1.0 / KVL, bias=eps_t[:, 0:1]
+            )
             live["rstd", q] = rstd
 
         def normalise(q):
@@ -296,16 +292,18 @@ def tile_multiheadlatentattention_pb_t_kernel(tc, x, w_kva, kva_norm_w, w_kvb, o
                 k_sb = outp.tile([P, 2, H, 256], F32, name="k_sb", tag="k_sb")
                 v_sb = outp.tile([P, 2, H * 128], F32, name="v_sb", tag="v_sb")
                 live["out", q] = (k_sb, v_sb)
-                r_pairs = live["r", q][:].rearrange("p t (j e) -> p t e j", e=2)
+                r_sb = work.tile([P, 2, R], F32, name="r_sb", tag="r_sb")
+                nc.vector.tensor_copy(out=r_sb[:], in_=live["r", q][:])
+                r_pairs = r_sb[:].rearrange("p t (j e) -> p t e j", e=2)
                 m1 = work.tile([P, 2, 2, 64], F32, name="m1", tag="m1")
-                nc.vector.tensor_tensor(
+                nc.gpsimd.tensor_tensor(
                     out=m1[:],
                     in0=r_pairs[:, :, 0:1, :].to_broadcast([P, 2, 2, 64]),
                     in1=tab1[:, t0 : t0 + 2, :, :],
                     op=ALU.mult,
                 )
                 m2 = work.tile([P, 2, 2, 64], F32, name="m2", tag="m2")
-                nc.vector.tensor_tensor(
+                nc.gpsimd.tensor_tensor(
                     out=m2[:],
                     in0=r_pairs[:, :, 1:2, :].to_broadcast([P, 2, 2, 64]),
                     in1=tab2[:, t0 : t0 + 2, :, :],

import math

import concourse.mybir as mybir
from concourse.masks import make_identity

F32 = mybir.dt.float32
BF16 = mybir.dt.bfloat16
I32 = mybir.dt.int32
U32 = mybir.dt.uint32
U8 = mybir.dt.uint8
FP8X4 = mybir.dt.float8_e4m3fn_x4
ALU = mybir.AluOpType
ACT = mybir.ActivationFunctionType

P = 128
B, T, C = 4, 1024, 1024
KVL, R, H = 512, 128, 4
TPP = 8
N_PAIRS = B * TPP // 2
EPS = 1e-6
RATIO = 10000.0 ** (-1.0 / 64.0)

FLOPS = 2 * B * T * C * (KVL + R) + 2 * B * T * KVL * (H * 256)


def tile_multiheadlatentattention_pb_t_kernel(tc, x, w_kva, kva_norm_w, w_kvb, out_0, out_1):
    nc = tc.nc
    with tc.tile_pool(name="const", bufs=1) as const, tc.tile_pool(name="xin", bufs=8) as xin, tc.tile_pool(
        name="stage", bufs=3
    ) as stage, tc.tile_pool(name="ring", bufs=7) as ring, tc.tile_pool(name="work", bufs=3) as work, tc.tile_pool(
        name="small", bufs=4
    ) as small, tc.psum_pool(name="psum", bufs=1) as psum, tc.manual_schedule():
        state = {"k": 0}

        def k_bank(shape, dtype, name):
            tag = "K%d" % (state["k"] % 4)
            state["k"] = state["k"] + 1
            return psum.tile(shape, dtype, name=name, tag=tag)

        engines = {"S": nc.scalar.copy, "V": nc.vector.tensor_copy}

        g_bc = const.tile([P, KVL], BF16, name="g_bc")

        waq = const.tile([P, 2 * 640], U32, name="waq", align_bytes=64)
        was = const.tile([P, 2 * 640], U8, name="was", align_bytes=64)
        wbq = const.tile([P, 1024], U32, name="wbq", align_bytes=64)
        wbs = const.tile([P, 1024], U8, name="wbs", align_bytes=64)
        tab1 = const.tile([P, TPP, 2, 64], F32, name="tab1")
        tab2 = const.tile([P, TPP, 2, 64], F32, name="tab2")
        ident_f = const.tile([P, P], F32, name="ident_f")
        ident_b = const.tile([P, P], BF16, name="ident_b")
        eps_t = const.tile([P, 1], F32, name="eps_t")
        sin_h = const.tile([P, TPP, 64], F32, name="sin_h")
        sin_q = const.tile([P, TPP, 64], F32, name="sin_q")
        sq_q = const.tile([P, TPP, 64], F32, name="sq_q")
        cos_h = const.tile([P, TPP, 64], F32, name="cos_h")
        sq_h = const.tile([P, TPP, 64], F32, name="sq_h")

        x_rows = x.rearrange("b (p t) k -> b p (t k)", t=TPP)
        k_rows = out_0.rearrange("b (p t) h d -> b p t (h d)", t=TPP)
        v_rows = out_1.rearrange("b (p t) h d -> b p t (h d)", t=TPP)
        x_words = []
        live = {}

        def transpose_words(src_words):
            xt = k_bank([P, 512], F32, "xt")
            for c in range(4):
                nc.tensor.transpose(
                    out=xt[:, P * c : P * c + P], in_=src_words[:, P * c : P * c + P], identity=ident_f[:]
                )
            return xt

        def copy_words(xt, dst_bf16, eng):
            engines[eng](
                out=dst_bf16.bitcast(F32).rearrange("p (g w u) -> p g w u", g=2, u=2),
                in_=xt[:].rearrange("p (g u w) -> p g w u", g=2, u=2),
            )

        with tc.tile_pool(name="setup", bufs=1) as setup:
            g_row = setup.tile([P, KVL], BF16, name="g_row")
            nc.vector.memset(g_row[:], 0.0)
            nc.scalar.dma_start(out=g_row[0:1, :], in_=kva_norm_w.rearrange("(o k) -> o k", o=1))
            ones = setup.tile([P, P], BF16, name="ones")
            nc.vector.memset(ones[:], 1.0)
            war = setup.tile([P, 5 * C], BF16, name="war")
            nc.sync.dma_start(
                out=war[:].rearrange("p (r k) -> p r k", r=5), in_=w_kva.rearrange("(r p) k -> p r k", p=P)
            )
            wbr = setup.tile([P, 8 * KVL], BF16, name="wbr")
            nc.sync.dma_start(
                out=wbr[:].rearrange("p (r k) -> p r k", r=8), in_=w_kvb.rearrange("(r p) k -> p r k", p=P)
            )
            for hb in range(8):
                xr = xin.tile([P, 4 * C], BF16, name="xr", tag="xr")
                nc.sync.dma_start(out=xr[:], in_=x_rows[hb // 2][:, 4 * C * (hb % 2) : 4 * C * (hb % 2) + 4 * C])
                x_words.append(xr[:].bitcast(F32))

            pos_i = setup.tile([P, TPP], I32, name="pos_i")
            nc.gpsimd.iota(pos_i[:], pattern=[[1, TPP]], base=0, channel_multiplier=TPP)
            make_identity(nc, ident_f[:])
            make_identity(nc, ident_b[:])
            nc.vector.memset(eps_t[:], EPS)
            pos_f = setup.tile([P, TPP], F32, name="pos_f")
            nc.vector.tensor_copy(out=pos_f[:], in_=pos_i[:])
            inv = setup.tile([P, 64], F32, name="inv")
            nc.vector.memset(inv[:, 0:1], 1.0)
            for s in range(6):
                n = 2**s
                nc.vector.tensor_scalar(
                    out=inv[:, n : 2 * n], in0=inv[:, 0:n], scalar1=RATIO**n, scalar2=None, op0=ALU.mult
                )
            turns = setup.tile([P, TPP, 64], F32, name="turns")
            nc.vector.scalar_tensor_tensor(
                out=turns[:],
                in0=pos_f[:].unsqueeze(2).to_broadcast([P, TPP, 64]),
                scalar=1.0 / (2.0 * math.pi),
                in1=inv[:].unsqueeze(1).to_broadcast([P, TPP, 64]),
                op0=ALU.mult,
                op1=ALU.mult,
            )
            whole_i = setup.tile([P, TPP, 64], I32, name="whole_i")
            nc.vector.tensor_copy(out=whole_i[:], in_=turns[:])
            whole_f = setup.tile([P, TPP, 64], F32, name="whole_f")
            nc.vector.tensor_copy(out=whole_f[:], in_=whole_i[:])
            frac = setup.tile([P, TPP, 64], F32, name="frac")
            nc.vector.tensor_tensor(out=frac[:], in0=turns[:], in1=whole_f[:], op=ALU.subtract)
            nc.scalar.activation(out=sin_h[:], in_=frac[:], func=ACT.Sin, scale=math.pi)
            nc.scalar.activation(out=sin_q[:], in_=frac[:], func=ACT.Sin, scale=0.5 * math.pi)

            war_w = war[:].bitcast(F32)
            for r in range(5):
                xt = transpose_words(war_w[:, 512 * r : 512 * r + 512])
                grp = stage.tile([P, 1024], BF16, name="grp", tag="cgrp", align_bytes=64)
                copy_words(xt, grp[:], "SV"[r % 2])
                for g in range(2):
                    cols = slice(640 * g + P * r, 640 * g + P * r + P)
                    nc.vector.quantize_mx(
                        out=waq[:, cols].bitcast(FP8X4), scales=was[:, cols], in_=grp[:, 512 * g : 512 * g + 512]
                    )
            for n, (ra, rb, dest) in enumerate(((0, 2, 0), (4, 6, 256), (1, 3, 512), (5, 7, 768))):
                wt = k_bank([P, 2, 4, P], BF16, "wt")
                for a, r in enumerate((ra, rb)):
                    for j in range(4):
                        nc.tensor.transpose(
                            out=wt[:, a, j, :],
                            in_=wbr[:, KVL * r + P * j : KVL * r + P * j + P],
                            identity=ident_b[:],
                        )
                grp = stage.tile([P, 1024], BF16, name="grp", tag="cgrp", align_bytes=64)
                engines["VS"[n % 2]](
                    out=grp[:].rearrange("p (a w j) -> p a w j", a=2, j=4),
                    in_=wt[:].rearrange("p a j w -> p a w j"),
                )
                nc.vector.quantize_mx(
                    out=wbq[:, dest : dest + 256].bitcast(FP8X4), scales=wbs[:, dest : dest + 256], in_=grp[:]
                )

            g_ps = k_bank([P, KVL], F32, "g_ps")
            nc.tensor.matmul(out=g_ps[:], lhsT=ones[:], rhs=g_row[:], start=True, stop=True)
            nc.scalar.copy(out=g_bc[:], in_=g_ps[:])

        def finish_tables():
            nc.scalar.activation(out=sq_q[:], in_=sin_q[:], func=ACT.Square)
            nc.scalar.activation(out=cos_h[:], in_=sq_q[:], func=ACT.Copy, scale=-2.0, bias=1.0)
            nc.scalar.activation(out=sq_h[:], in_=sin_h[:], func=ACT.Square)
            nc.scalar.activation(out=tab1[:, :, 0, :], in_=sq_h[:], func=ACT.Copy, scale=-2.0, bias=1.0)
            nc.scalar.activation(out=tab2[:, :, 1, :], in_=sq_h[:], func=ACT.Copy, scale=-2.0, bias=1.0)
            nc.vector.scalar_tensor_tensor(
                out=tab1[:, :, 1, :], in0=sin_h[:], scalar=2.0, in1=cos_h[:], op0=ALU.mult, op1=ALU.mult
            )
            nc.vector.scalar_tensor_tensor(
                out=tab2[:, :, 0, :], in0=sin_h[:], scalar=-2.0, in1=cos_h[:], op0=ALU.mult, op1=ALU.mult
            )

        def x_transpose(q):
            live["xt", q] = [
                transpose_words(x_words[(2 * q + a) // 4][:, 512 * ((2 * q + a) % 4) : 512 * ((2 * q + a) % 4) + 512])
                for a in range(2)
            ]

        def x_copy(q):
            xg = stage.tile([P, 2048], BF16, name="xg", tag="xgrp", align_bytes=64)
            for a in range(2):
                copy_words(live["xt", q][a], xg[:, 1024 * a : 1024 * a + 1024], "SV"[a])
            live["xg", q] = xg

        def x_quantise(q):
            xq = ring.tile([P, 512], U32, name="xq", tag="xq", align_bytes=64)
            xs = ring.tile([P, 512], U8, name="xs", tag="xs", align_bytes=64)
            nc.vector.quantize_mx(out=xq[:].bitcast(FP8X4), scales=xs[:], in_=live["xg", q][:])
            live["xq", q] = (xq, xs)

        def stage1_pass(out, q, a, g, lo, hi):
            xq, xs = live["xq", q]
            xc = slice(256 * a + P * g, 256 * a + P * g + P)
            nc.tensor.matmul_mx(
                out=out,
                lhsT=xq[:, xc].bitcast(FP8X4),
                lhsT_scale=xs[:, xc],
                rhs=waq[:, 640 * g + lo : 640 * g + hi].bitcast(FP8X4),
                rhs_scale=was[:, 640 * g + lo : 640 * g + hi],
                start=(g == 0),
                stop=(g == 1),
            )

        def stage1_latent(q):
            tiles = []
            for a in range(2):
                l = psum.tile([P, KVL], F32, name="l", tag="L%d" % a)
                for g in range(2):
                    stage1_pass(l[:], q, a, g, 0, KVL)
                tiles.append(l)
            live["l", q] = tiles

        def stage1_rotary(q):
            r_ps = psum.tile([P, 2, R], F32, name="r_ps", tag="R")
            for a in range(2):
                for g in range(2):
                    stage1_pass(r_ps[:, a, :], q, a, g, KVL, KVL + R)
            live["r", q] = r_ps

        def squares(q):
            ssq = small.tile([P, 2], F32, name="ssq", tag="ssq")
            for a in range(2):
                junk = work.tile([P, KVL], BF16, name="junk", tag="junk", bufs=2)
                nc.scalar.activation(out=junk[:], in_=live["l", q][a][:], func=ACT.Square, accum_out=ssq[:, a : a + 1])
            rstd = small.tile([P, 2], F32, name="rstd", tag="rstd")
            nc.scalar.activation(
                out=rstd[:], in_=ssq[:], func=ACT.Abs_reciprocal_sqrt, scale=1.0 / KVL, bias=eps_t[:, 0:1]
            )
            live["rstd", q] = rstd

        def normalise(q):
            rstd = live["rstd", q]
            c_sb = work.tile([P, 2, KVL], BF16, name="c_sb", tag="c_sb")
            for a in range(2):
                nc.vector.scalar_tensor_tensor(
                    out=c_sb[:, a, :],
                    in0=live["l", q][a][:],
                    scalar=rstd[:, a : a + 1],
                    in1=g_bc[:],
                    op0=ALU.mult,
                    op1=ALU.mult,
                )
            live["c", q] = c_sb

        def c_transpose(q):
            ct = psum.tile([P, 2, 4, P], BF16, name="ct", tag="C")
            for a in range(2):
                for j in range(4):
                    nc.tensor.transpose(
                        out=ct[:, a, j, :], in_=live["c", q][:, a, P * j : P * j + P], identity=ident_b[:]
                    )
            live["ct", q] = ct

        def c_copy(q):
            grp = stage.tile([P, 1024], BF16, name="grp", tag="cgrp", align_bytes=64)
            nc.scalar.copy(
                out=grp[:].rearrange("p (a w j) -> p a w j", a=2, j=4),
                in_=live["ct", q][:].rearrange("p a j w -> p a w j"),
            )
            live["cg", q] = grp

        def c_quantise(q):
            cq = work.tile([P, 256], U32, name="cq", tag="cq", align_bytes=64)
            cs = work.tile([P, 256], U8, name="cs", tag="cs", align_bytes=64)
            nc.vector.quantize_mx(out=cq[:].bitcast(FP8X4), scales=cs[:], in_=live["cg", q][:])
            live["cq", q] = (cq, cs)

        def stage2(q):
            cq, cs = live["cq", q]
            banks = []
            for a in range(2):
                for part in range(2):
                    kv = k_bank([P, 512], F32, "kv")
                    nc.tensor.matmul_mx(
                        out=kv[:],
                        lhsT=cq[:, P * a : P * a + P].bitcast(FP8X4),
                        lhsT_scale=cs[:, P * a : P * a + P],
                        rhs=wbq[:, 512 * part : 512 * part + 512].bitcast(FP8X4),
                        rhs_scale=wbs[:, 512 * part : 512 * part + 512],
                        start=True,
                        stop=True,
                    )
                    banks.append(kv)
            live["kv", q] = banks

        with tc.tile_pool(name="outp", bufs=6) as outp:

            def rotate(q):
                t0 = 2 * (q % 4)
                k_sb = outp.tile([P, 2, H, 256], F32, name="k_sb", tag="k_sb")
                v_sb = outp.tile([P, 2, H * 128], F32, name="v_sb", tag="v_sb")
                live["out", q] = (k_sb, v_sb)
                r_sb = work.tile([P, 2, R], F32, name="r_sb", tag="r_sb")
                nc.vector.tensor_copy(out=r_sb[:], in_=live["r", q][:])
                r_pairs = r_sb[:].rearrange("p t (j e) -> p t e j", e=2)
                m1 = work.tile([P, 2, 2, 64], F32, name="m1", tag="m1")
                nc.gpsimd.tensor_tensor(
                    out=m1[:],
                    in0=r_pairs[:, :, 0:1, :].to_broadcast([P, 2, 2, 64]),
                    in1=tab1[:, t0 : t0 + 2, :, :],
                    op=ALU.mult,
                )
                m2 = work.tile([P, 2, 2, 64], F32, name="m2", tag="m2")
                nc.gpsimd.tensor_tensor(
                    out=m2[:],
                    in0=r_pairs[:, :, 1:2, :].to_broadcast([P, 2, 2, 64]),
                    in1=tab2[:, t0 : t0 + 2, :, :],
                    op=ALU.mult,
                )
                nc.gpsimd.tensor_tensor(
                    out=k_sb[:, :, 0, 128:256].rearrange("p t (j e) -> p t j e", e=2),
                    in0=m1[:].rearrange("p t e j -> p t j e"),
                    in1=m2[:].rearrange("p t e j -> p t j e"),
                    op=ALU.add,
                )
                nc.gpsimd.tensor_scalar(
                    out=k_sb[:, :, 1:4, 128:256],
                    in0=k_sb[:, :, 0:1, 128:256].to_broadcast([P, 2, 3, 128]),
                    scalar1=1.0,
                    scalar2=0.0,
                    op0=ALU.mult,
                    op1=ALU.add,
                )

            def copy_out(q):
                k_sb, v_sb = live["out", q]
                for a in range(2):
                    eng = engines["SV"[a]]
                    eng(out=k_sb[:, a, :, 0:128], in_=live["kv", q][2 * a][:].rearrange("p (h d) -> p h d", h=H))
                    eng(out=v_sb[:, a, :], in_=live["kv", q][2 * a + 1][:])

            def store(q):
                k_sb, v_sb = live["out", q]
                b = q // 4
                t0 = 2 * (q % 4)
                nc.sync.dma_start(out=k_rows[b][:, t0 : t0 + 2, :], in_=k_sb[:].rearrange("p t h d -> p t (h d)"))
                nc.sync.dma_start(out=v_rows[b][:, t0 : t0 + 2, :], in_=v_sb[:])

            def is_pair(q):
                return 0 <= q < N_PAIRS

            x_transpose(0)
            x_copy(0)
            x_quantise(0)
            next_x = 1
            for n in range(N_PAIRS + 3):
                fresh = [q for q in range(next_x, next_x + (2 if n < 3 else 1)) if is_pair(q)]
                next_x = next_x + len(fresh)
                for q in fresh:
                    x_transpose(q)
                if is_pair(n - 2):
                    c_transpose(n - 2)
                if is_pair(n - 1):
                    squares(n - 1)
                for q in fresh:
                    x_copy(q)
                if is_pair(n - 1):
                    normalise(n - 1)
                if is_pair(n - 2):
                    c_copy(n - 2)
                    c_quantise(n - 2)
                for q in fresh:
                    x_quantise(q)
                if n == 0:
                    finish_tables()
                if is_pair(n - 3):
                    stage2(n - 3)
                if is_pair(n - 1):
                    stage1_rotary(n - 1)
                if is_pair(n):
                    stage1_latent(n)
                if is_pair(n - 1):
                    rotate(n - 1)
                if is_pair(n - 3):
                    copy_out(n - 3)
                    store(n - 3)
